import numpy as np
import ml_dtypes


def mxq(x, axis, fmt="e4m3"):
    dtype, down = {"e4m3": (ml_dtypes.float8_e4m3fn, 7), "e5m2": (ml_dtypes.float8_e5m2, 14)}[fmt]
    v = np.moveaxis(np.asarray(x, np.float32).astype(ml_dtypes.bfloat16).astype(np.float64), axis, -1)
    blocks = v.reshape(v.shape[:-1] + (-1, 32))
    amax = np.abs(blocks).max(-1, keepdims=True)
    byte = np.maximum(np.where(amax > 0, np.frexp(amax)[1] - 1 + 127, 0) - down, 1)
    scale = np.exp2(byte - 127.0)
    codes = (blocks / scale).astype(np.float32).astype(dtype).astype(np.float64)
    return np.moveaxis((codes * scale).reshape(v.shape), -1, axis)


WIDE = False


def mx_kscale(k):
    if not WIDE:
        return np.ones(k)
    levels = np.array([10, -10, 5, -5, 0])
    a = np.random.permutation(np.resize(levels, k // 512 * 4)).reshape(k // 512, 4)
    idx = np.arange(k)
    return np.exp2(a[idx // 512, idx % 128 // 32])


BF16 = ml_dtypes.bfloat16


def bf(x):
    return np.asarray(x, np.float32).astype(BF16)


def f64(x):
    return np.asarray(x).astype(np.float64)


E2M1 = np.array([0.0, 0.5, 1.0, 1.5, 2.0, 3.0, 4.0, 6.0, -0.0, -0.5, -1.0, -1.5, -2.0, -3.0, -4.0, -6.0])


def pack_weight(w, fmt):
    k, n = w.shape
    w = f64(bf(w)).reshape(k // 32, 32, n)
    amax = np.abs(w).max(1)
    if fmt == "e4m3":
        byte = np.frexp(amax)[1] - 1 + 127 - 7
    else:
        mant, ex = np.frexp(amax / 6.0)
        byte = np.where(mant > 0.5, ex, ex - 1) + 127
    byte = np.clip(np.where(amax > 0, byte, 1), 1, 254)
    scaled = (w * np.exp2(127.0 - byte)[:, None, :]).reshape(k, n).astype(np.float32)
    by_word = np.ascontiguousarray(scaled.reshape(k // 512, 128, 4, n).transpose(0, 1, 3, 2))
    if fmt == "e4m3":
        words = by_word.astype(ml_dtypes.float8_e4m3fn).view(np.uint8)
    else:
        c = by_word.astype(ml_dtypes.float4_e2m1fn).view(np.uint8) & 0xF
        words = c[..., 0::2] | (c[..., 1::2] << 4)
    return np.ascontiguousarray(words), np.ascontiguousarray(byte.astype(np.uint8).reshape(k // 512, 16, n))


def unpack_weight(words, scales, fmt):
    g, p, n, _ = words.shape
    if fmt == "e4m3":
        vals = np.ascontiguousarray(words).view(ml_dtypes.float8_e4m3fn).astype(np.float64)
    else:
        nib = np.empty((g, p, n, 4), np.uint8)
        nib[..., 0::2] = words & 0xF
        nib[..., 1::2] = words >> 4
        vals = E2M1[nib]
    vals = vals * np.repeat(np.exp2(scales.astype(np.float64) - 127.0), 8, axis=1)[..., None]
    return vals.transpose(0, 1, 3, 2).reshape(g * 512, n)

def pack4(w):
    words, scales = pack_weight(w, "e2m1")
    return words.reshape(words.shape[0], 128, -1), scales


def unpack4(words, scales):
    return unpack_weight(words.reshape(words.shape[0], 128, -1, 2), scales, "e2m1")


B, D, K, L = 4096, 512, 1024, 4
A = 25.0


def setup_inputs():
    s = mx_kscale(D)
    z0 = bf(np.random.standard_normal((B, D)) * s)
    W = np.random.standard_normal((D, D)) * np.sqrt(A) / D / s[None, :]
    W_words, W_scales = pack4(W.T)
    cb = bf(np.random.standard_normal((K, D)) * np.sqrt(A / D))
    return {"z0": z0, "W_words": W_words, "W_scales": W_scales, "cb": cb}


def reference(z0, W_words, W_scales, cb):
    c = f64(cb)
    z = mxq(f64(z0), 1, "e4m3") @ unpack4(W_words, W_scales)
    z_sq = np.sum(z * z, axis=-1, keepdims=True)
    c_sq = np.sum(c * c, axis=-1)[None, :]
    dists = z_sq + c_sq - 2.0 * (mxq(z, 1, "e4m3") @ mxq(c, 1, "e4m3").T)
    return z, dists

@@ -1,0 +1,266 @@
+from contextlib import ExitStack
+
+import concourse.mybir as mybir
+from concourse.masks import make_identity
+
+F32 = mybir.dt.float32
+BF16 = mybir.dt.bfloat16
+I32 = mybir.dt.int32
+U32 = mybir.dt.uint32
+U8 = mybir.dt.uint8
+FP8X4 = mybir.dt.float8_e4m3fn_x4
+FP4X4 = mybir.dt.float4_e2m1fn_x4
+ADD = mybir.AluOpType.add
+SQUARE = mybir.ActivationFunctionType.Square
+
+P = 128
+PACK = 4
+B, D, K = 4096, 512, 1024
+BANK = 512
+TILES_PER_BLOCK = 4
+BLOCK = P * TILES_PER_BLOCK
+N_BLOCKS = B // BLOCK
+N_TILES = B // P
+CB_TILES = K // P
+CODE_HALVES = K // BANK
+LAG = 2
+
+FLOPS = 2 * B * D * D + 2 * B * D * K
+
+
+def tile_softresidualvq_pa_t_kernel(tc, z0, W_words, W_scales, cb, out_0, out_1):
+    nc = tc.nc
+    with ExitStack() as ctx:
+        const = ctx.enter_context(tc.tile_pool(name="const", bufs=1))
+        z0_pool = ctx.enter_context(tc.tile_pool(name="z0", bufs=N_BLOCKS))
+        z0q_pool = ctx.enter_context(tc.tile_pool(name="z0q", bufs=2))
+        zq_pool = ctx.enter_context(tc.tile_pool(name="zq", bufs=4))
+        out_pool = ctx.enter_context(tc.tile_pool(name="out", bufs=3))
+        scratch = ctx.enter_context(tc.tile_pool(name="scratch", bufs=4))
+        psum = ctx.enter_context(tc.psum_pool(name="psum", bufs=2))
+
+        def block_rows(dram, j):
+            return dram[j * BLOCK : (j + 1) * BLOCK, :].rearrange(
+                "(p s) d -> p s d", s=TILES_PER_BLOCK
+            )
+
+        z0_sb = {}
+
+        def load_z0(j):
+            rows = z0_pool.tile([P, TILES_PER_BLOCK, D], BF16, name="z0_rows")
+            nc.sync.dma_start(out=rows[:], in_=block_rows(z0, j))
+            z0_sb[j] = rows
+
+        w_words = const.tile([P, 2 * D], U8, align_bytes=64)
+        w_scales = const.tile([P, D], U8, align_bytes=64)
+        nc.vector.memset(w_scales[:].bitcast(I32), 0)
+
+        load_z0(0)
+        nc.sync.dma_start(out=w_words[:].bitcast(I32), in_=W_words[0].bitcast(I32))
+        for q in range(4):
+            nc.sync.dma_start(
+                out=w_scales[32 * q : 32 * q + 4, :].bitcast(I32),
+                in_=W_scales[0, 4 * q : 4 * q + 4, :].bitcast(I32),
+            )
+        cb_sb = const.tile([P, CB_TILES, D], BF16)
+        nc.sync.dma_start(out=cb_sb[:], in_=cb.rearrange("(r p) d -> p r d", p=P))
+        for j in range(1, N_BLOCKS):
+            load_z0(j)
+
+        ident_f32 = const.tile([P, P], F32)
+        make_identity(nc, ident_f32[:])
+        ident_bf16 = const.tile([P, P], BF16)
+        make_identity(nc, ident_bf16[:])
+
+        z0_grouped = {}
+        z0_codes = {}
+        z0_scales = {}
+
+        def transpose_block(j):
+            grouped = z0q_pool.tile([P, BLOCK * PACK], BF16, name="z0_grouped", align_bytes=64)
+            words = grouped[:].bitcast(F32).rearrange(
+                "p (h s b u) -> p h s b u", h=2, s=2, u=2
+            )
+            for h in range(2):
+                z0T_ps = psum.tile([P, 2, 2, P], F32, tag="z0T")
+                for s in range(2):
+                    z0_words = z0_sb[j][:, 2 * h + s, :].bitcast(F32)
+                    for u in range(2):
+                        nc.tensor.transpose(
+                            z0T_ps[:, s, u, :], z0_words[:, u : D // 2 : 2], ident_f32[:]
+                        )
+                nc.scalar.copy(
+                    out=words[:, h], in_=z0T_ps[:].rearrange("p s u b -> p s b u")
+                )
+            z0_grouped[j] = grouped
+
+        def quantise_z0(j):
+            codes = z0q_pool.tile([P, BLOCK], U32, name="z0_codes", align_bytes=64)
+            scales = z0q_pool.tile([P, BLOCK], U8, name="z0_scales", align_bytes=64)
+            nc.vector.quantize_mx(
+                out=codes[:].bitcast(FP8X4), scales=scales[:], in_=z0_grouped[j][:]
+            )
+            z0_codes[j] = codes
+            z0_scales[j] = scales
+
+        cb_codes = const.tile([P, K], U32, align_bytes=64)
+        cb_scales = const.tile([P, K], U8, align_bytes=64)
+        c_sq = const.tile([P, K], F32)
+
+        def prepare_codebook():
+            grouped = const.tile([P, K, PACK], BF16, name="cb_grouped", align_bytes=64)
+            for pair in range(CB_TILES // 2):
+                cbT_ps = psum.tile([P, 2, PACK, P], BF16, tag="dist")
+                for r in range(2):
+                    for t in range(PACK):
+                        nc.tensor.transpose(
+                            cbT_ps[:, r, t, :],
+                            cb_sb[:, 2 * pair + r, t * P : (t + 1) * P],
+                            ident_bf16[:],
+                        )
+                nc.vector.tensor_scalar_mul(
+                    out=grouped[:, 2 * pair * P : (2 * pair + 2) * P, :].rearrange(
+                        "p (r k) t -> p r k t", r=2
+                    ),
+                    in0=cbT_ps[:].rearrange("p r t k -> p r k t"),
+                    scalar1=-2.0,
+                )
+            for h in range(CODE_HALVES):
+                half = slice(h * BANK, (h + 1) * BANK)
+                nc.vector.quantize_mx(
+                    out=cb_codes[:, half].bitcast(FP8X4),
+                    scales=cb_scales[:, half],
+                    in_=grouped[:, half, :].rearrange("p k t -> p (k t)"),
+                )
+
+        def prepare_code_norms():
+            by_partition = const.tile([P, CB_TILES], F32, name="c_sq_by_partition")
+            for r in range(CB_TILES):
+                squares = scratch.tile([P, D], F32, name="squares")
+                nc.scalar.activation(
+                    out=squares[:],
+                    in_=cb_sb[:, r, :],
+                    func=SQUARE,
+                    accum_out=by_partition[:, r : r + 1],
+                )
+            repeated = const.tile([P, CB_TILES, P], F32, name="c_sq_repeated")
+            nc.vector.tensor_copy(
+                out=repeated[:],
+                in_=by_partition[:].unsqueeze(2).to_broadcast([P, CB_TILES, P]),
+            )
+            for h in range(CODE_HALVES):
+                c_sq_ps = psum.tile([P, BANK // P, P], F32, tag="z")
+                for r in range(BANK // P):
+                    nc.tensor.transpose(
+                        c_sq_ps[:, r, :], repeated[:, h * (BANK // P) + r, :], ident_f32[:]
+                    )
+                nc.vector.tensor_copy(
+                    out=c_sq[:, h * BANK : (h + 1) * BANK],
+                    in_=c_sq_ps[:].rearrange("p r k -> p (r k)"),
+                )
+
+        z_out = {}
+        z_sq = {}
+        z_grouped = {}
+        z_codes = {}
+        z_scales = {}
+
+        def whiten_tile(tau):
+            j, s = divmod(tau, TILES_PER_BLOCK)
+            rows = slice(s * P, (s + 1) * P)
+            if s == 0:
+                z_out[j] = out_pool.tile([P, TILES_PER_BLOCK, D], F32, name="z_out")
+                z_sq[j] = out_pool.tile([P, TILES_PER_BLOCK], F32, name="z_sq")
+
+            zT_ps = psum.tile([P, PACK, P], F32, tag="zT")
+            for t in range(PACK):
+                nc.tensor.matmul_mx(
+                    out=zT_ps[:, t, :],
+                    lhsT=w_words[:, 2 * t * P : 2 * (t + 1) * P].bitcast(FP4X4),
+                    lhsT_scale=w_scales[:, t * P : (t + 1) * P],
+                    rhs=z0_codes[j][:, rows].bitcast(FP8X4),
+                    rhs_scale=z0_scales[j][:, rows],
+                    start=True,
+                    stop=True,
+                )
+            grouped = zq_pool.tile([P, P, PACK], BF16, name="z_grouped", align_bytes=64)
+            if tau % 2 == 0:
+                nc.scalar.copy(out=grouped[:], in_=zT_ps[:].rearrange("p t b -> p b t"))
+            else:
+                nc.vector.tensor_copy(out=grouped[:], in_=zT_ps[:].rearrange("p t b -> p b t"))
+            z_grouped[tau] = grouped
+
+            z_ps = psum.tile([P, D], F32, tag="z")
+            nc.tensor.matmul_mx(
+                out=z_ps[:],
+                lhsT=z0_codes[j][:, rows].bitcast(FP8X4),
+                lhsT_scale=z0_scales[j][:, rows],
+                rhs=w_words[:].bitcast(FP4X4),
+                rhs_scale=w_scales[:],
+                start=True,
+                stop=True,
+            )
+            nc.scalar.copy(out=z_out[j][:, s, :], in_=z_ps[:])
+            squares = scratch.tile([P, D], F32, name="squares")
+            nc.scalar.activation(
+                out=squares[:], in_=z_ps[:], func=SQUARE, accum_out=z_sq[j][:, s : s + 1]
+            )
+            if s == TILES_PER_BLOCK - 1:
+                nc.sync.dma_start(out=block_rows(out_0, j), in_=z_out[j][:])
+
+        def quantise_z(tau):
+            codes = zq_pool.tile([P, P], U32, name="z_codes", align_bytes=64)
+            scales = zq_pool.tile([P, P], U8, name="z_scales", align_bytes=64)
+            nc.vector.quantize_mx(
+                out=codes[:].bitcast(FP8X4),
+                scales=scales[:],
+                in_=z_grouped[tau][:].rearrange("p b t -> p (b t)"),
+            )
+            z_codes[tau] = codes
+            z_scales[tau] = scales
+
+        d_out = {}
+
+        def distance_tile(tau):
+            j, s = divmod(tau, TILES_PER_BLOCK)
+            if s == 0:
+                d_out[j] = out_pool.tile([P, TILES_PER_BLOCK, K], F32, name="d_out")
+            for h in range(CODE_HALVES):
+                half = slice(h * BANK, (h + 1) * BANK)
+                dist_ps = psum.tile([P, BANK], F32, tag="dist")
+                nc.tensor.matmul_mx(
+                    out=dist_ps[:],
+                    lhsT=z_codes[tau][:].bitcast(FP8X4),
+                    lhsT_scale=z_scales[tau][:],
+                    rhs=cb_codes[:, half].bitcast(FP8X4),
+                    rhs_scale=cb_scales[:, half],
+                    start=True,
+                    stop=True,
+                )
+                nc.vector.scalar_tensor_tensor(
+                    out=d_out[j][:, s, half],
+                    in0=dist_ps[:],
+                    scalar=z_sq[j][:, s : s + 1],
+                    in1=c_sq[:, half],
+                    op0=ADD,
+                    op1=ADD,
+                )
+            if s == TILES_PER_BLOCK - 1:
+                nc.sync.dma_start(out=block_rows(out_1, j), in_=d_out[j][:])
+
+        transpose_block(0)
+        quantise_z0(0)
+        prepare_codebook()
+        prepare_code_norms()
+        for tau in range(N_TILES + LAG):
+            j, s = divmod(tau, TILES_PER_BLOCK)
+            if s == 0 and j + 1 < N_BLOCKS:
+                transpose_block(j + 1)
+            if tau < N_TILES:
+                whiten_tile(tau)
+            if s == TILES_PER_BLOCK // 2 and j + 1 < N_BLOCKS:
+                quantise_z0(j + 1)
+            if 1 <= tau <= N_TILES:
+                quantise_z(tau - 1)
+            if tau >= LAG:
+                distance_tile(tau - LAG)

@@ -18,6 +18,7 @@ PACK = 4
 B, D, K = 4096, 512, 1024
 BANK = 512
 TILES_PER_BLOCK = 4
+TILES_PER_STORE = 2
 BLOCK = P * TILES_PER_BLOCK
 N_BLOCKS = B // BLOCK
 N_TILES = B // P
@@ -43,6 +44,11 @@ def tile_softresidualvq_pa_t_kernel(tc, z0, W_words, W_scales, cb, out_0, out_1)
             return dram[j * BLOCK : (j + 1) * BLOCK, :].rearrange(
                 "(p s) d -> p s d", s=TILES_PER_BLOCK
             )
+
+        def store_finished_tiles(dram, block_sb, j, s):
+            if (s + 1) % TILES_PER_STORE == 0:
+                tiles = slice(s + 1 - TILES_PER_STORE, s + 1)
+                nc.sync.dma_start(out=block_rows(dram, j)[:, tiles, :], in_=block_sb[:, tiles, :])
 
         z0_sb = {}
 
@@ -133,20 +139,23 @@ def tile_softresidualvq_pa_t_kernel(tc, z0, W_words, W_scales, cb, out_0, out_1)
                     in_=grouped[:, half, :].rearrange("p k t -> p (k t)"),
                 )
 
-        def prepare_code_norms():
-            by_partition = const.tile([P, CB_TILES], F32, name="c_sq_by_partition")
+        c_sq_by_partition = const.tile([P, CB_TILES], F32)
+
+        def square_codebook():
             for r in range(CB_TILES):
                 squares = scratch.tile([P, D], F32, name="squares")
                 nc.scalar.activation(
                     out=squares[:],
                     in_=cb_sb[:, r, :],
                     func=SQUARE,
-                    accum_out=by_partition[:, r : r + 1],
+                    accum_out=c_sq_by_partition[:, r : r + 1],
                 )
+
+        def spread_code_norms():
             repeated = const.tile([P, CB_TILES, P], F32, name="c_sq_repeated")
             nc.vector.tensor_copy(
                 out=repeated[:],
-                in_=by_partition[:].unsqueeze(2).to_broadcast([P, CB_TILES, P]),
+                in_=c_sq_by_partition[:].unsqueeze(2).to_broadcast([P, CB_TILES, P]),
             )
             for h in range(CODE_HALVES):
                 c_sq_ps = psum.tile([P, BANK // P, P], F32, tag="z")
@@ -205,8 +214,7 @@ def tile_softresidualvq_pa_t_kernel(tc, z0, W_words, W_scales, cb, out_0, out_1)
             nc.scalar.activation(
                 out=squares[:], in_=z_ps[:], func=SQUARE, accum_out=z_sq[j][:, s : s + 1]
             )
-            if s == TILES_PER_BLOCK - 1:
-                nc.sync.dma_start(out=block_rows(out_0, j), in_=z_out[j][:])
+            store_finished_tiles(out_0, z_out[j], j, s)
 
         def quantise_z(tau):
             codes = zq_pool.tile([P, P], U32, name="z_codes", align_bytes=64)
@@ -245,22 +253,24 @@ def tile_softresidualvq_pa_t_kernel(tc, z0, W_words, W_scales, cb, out_0, out_1)
                     op0=ADD,
                     op1=ADD,
                 )
-            if s == TILES_PER_BLOCK - 1:
-                nc.sync.dma_start(out=block_rows(out_1, j), in_=d_out[j][:])
+            store_finished_tiles(out_1, d_out[j], j, s)
 
-        transpose_block(0)
-        quantise_z0(0)
-        prepare_codebook()
-        prepare_code_norms()
-        for tau in range(N_TILES + LAG):
-            j, s = divmod(tau, TILES_PER_BLOCK)
-            if s == 0 and j + 1 < N_BLOCKS:
-                transpose_block(j + 1)
-            if tau < N_TILES:
-                whiten_tile(tau)
-            if s == TILES_PER_BLOCK // 2 and j + 1 < N_BLOCKS:
-                quantise_z0(j + 1)
-            if 1 <= tau <= N_TILES:
-                quantise_z(tau - 1)
-            if tau >= LAG:
-                distance_tile(tau - LAG)
+        with tc.manual_schedule():
+            transpose_block(0)
+            quantise_z0(0)
+            prepare_codebook()
+            square_codebook()
+            for tau in range(N_TILES + LAG):
+                j, s = divmod(tau, TILES_PER_BLOCK)
+                if s == 0 and j + 1 < N_BLOCKS:
+                    transpose_block(j + 1)
+                if tau < N_TILES:
+                    whiten_tile(tau)
+                if s == TILES_PER_BLOCK - 1 and j + 1 < N_BLOCKS:
+                    quantise_z0(j + 1)
+                if 1 <= tau <= N_TILES:
+                    quantise_z(tau - 1)
+                if tau == LAG:
+                    spread_code_norms()
+                if tau >= LAG:
+                    distance_tile(tau - LAG)

@@ -11,6 +11,7 @@ U8 = mybir.dt.uint8
 FP8X4 = mybir.dt.float8_e4m3fn_x4
 FP4X4 = mybir.dt.float4_e2m1fn_x4
 ADD = mybir.AluOpType.add
+MULT = mybir.AluOpType.mult
 SQUARE = mybir.ActivationFunctionType.Square
 
 P = 128
@@ -18,13 +19,13 @@ PACK = 4
 B, D, K = 4096, 512, 1024
 BANK = 512
 TILES_PER_BLOCK = 4
-TILES_PER_STORE = 2
 BLOCK = P * TILES_PER_BLOCK
 N_BLOCKS = B // BLOCK
 N_TILES = B // P
+N_PAIRS = N_TILES // 2
 CB_TILES = K // P
 CODE_HALVES = K // BANK
-LAG = 2
+WORDS = D // 2
 
 FLOPS = 2 * B * D * D + 2 * B * D * K
 
@@ -34,34 +35,38 @@ def tile_softresidualvq_pa_t_kernel(tc, z0, W_words, W_scales, cb, out_0, out_1)
     with ExitStack() as ctx:
         const = ctx.enter_context(tc.tile_pool(name="const", bufs=1))
         z0_pool = ctx.enter_context(tc.tile_pool(name="z0", bufs=N_BLOCKS))
-        z0q_pool = ctx.enter_context(tc.tile_pool(name="z0q", bufs=2))
-        zq_pool = ctx.enter_context(tc.tile_pool(name="zq", bufs=4))
+        stage = ctx.enter_context(tc.tile_pool(name="stage", bufs=3))
+        zb_pool = ctx.enter_context(tc.tile_pool(name="zb", bufs=6))
         out_pool = ctx.enter_context(tc.tile_pool(name="out", bufs=3))
         scratch = ctx.enter_context(tc.tile_pool(name="scratch", bufs=4))
-        psum = ctx.enter_context(tc.psum_pool(name="psum", bufs=2))
+        psum_t = ctx.enter_context(tc.psum_pool(name="psum_t", bufs=2))
+        psum_z = ctx.enter_context(tc.psum_pool(name="psum_z", bufs=2))
+        psum_d = ctx.enter_context(tc.psum_pool(name="psum_d", bufs=4))
 
         def block_rows(dram, j):
             return dram[j * BLOCK : (j + 1) * BLOCK, :].rearrange(
                 "(p s) d -> p s d", s=TILES_PER_BLOCK
             )
 
-        def store_finished_tiles(dram, block_sb, j, s):
-            if (s + 1) % TILES_PER_STORE == 0:
-                tiles = slice(s + 1 - TILES_PER_STORE, s + 1)
-                nc.sync.dma_start(out=block_rows(dram, j)[:, tiles, :], in_=block_sb[:, tiles, :])
+        def store_tiles(dram, block_sb, j, first, last):
+            tiles = slice(first, last + 1)
+            nc.sync.dma_start(out=block_rows(dram, j)[:, tiles, :], in_=block_sb[:, tiles, :])
 
         z0_sb = {}
 
-        def load_z0(j):
+        def load_z0(j, pieces):
             rows = z0_pool.tile([P, TILES_PER_BLOCK, D], BF16, name="z0_rows")
-            nc.sync.dma_start(out=rows[:], in_=block_rows(z0, j))
+            step = TILES_PER_BLOCK // pieces
+            for c in range(pieces):
+                tiles = slice(c * step, (c + 1) * step)
+                nc.sync.dma_start(out=rows[:, tiles, :], in_=block_rows(z0, j)[:, tiles, :])
             z0_sb[j] = rows
 
         w_words = const.tile([P, 2 * D], U8, align_bytes=64)
         w_scales = const.tile([P, D], U8, align_bytes=64)
         nc.vector.memset(w_scales[:].bitcast(I32), 0)
 
-        load_z0(0)
+        load_z0(0, 2)
         nc.sync.dma_start(out=w_words[:].bitcast(I32), in_=W_words[0].bitcast(I32))
         for q in range(4):
             nc.sync.dma_start(
@@ -71,75 +76,75 @@ def tile_softresidualvq_pa_t_kernel(tc, z0, W_words, W_scales, cb, out_0, out_1)
         cb_sb = const.tile([P, CB_TILES, D], BF16)
         nc.sync.dma_start(out=cb_sb[:], in_=cb.rearrange("(r p) d -> p r d", p=P))
         for j in range(1, N_BLOCKS):
-            load_z0(j)
+            load_z0(j, 1)
 
         ident_f32 = const.tile([P, P], F32)
         make_identity(nc, ident_f32[:])
-        ident_bf16 = const.tile([P, P], BF16)
-        make_identity(nc, ident_bf16[:])
 
+        def copy_on(engine, out, in_):
+            if engine == "scalar":
+                nc.scalar.copy(out=out, in_=in_)
+            else:
+                nc.vector.tensor_copy(out=out, in_=in_)
+
+        def transpose_words(bank, slot, rows_bf16):
+            words = rows_bf16.bitcast(F32)
+            for u in range(2):
+                nc.tensor.transpose(bank[:, slot, u, :], words[:, u:WORDS:2], ident_f32[:])
+
+        def interleave(engine, grouped_bf16, bank):
+            copy_on(
+                engine,
+                grouped_bf16.bitcast(F32).rearrange("p (s b u) -> p s b u", s=2, u=2),
+                bank[:].rearrange("p s u b -> p s b u"),
+            )
+
+        z0T = {}
         z0_grouped = {}
         z0_codes = {}
         z0_scales = {}
 
-        def transpose_block(j):
-            grouped = z0q_pool.tile([P, BLOCK * PACK], BF16, name="z0_grouped", align_bytes=64)
-            words = grouped[:].bitcast(F32).rearrange(
-                "p (h s b u) -> p h s b u", h=2, s=2, u=2
-            )
-            for h in range(2):
-                z0T_ps = psum.tile([P, 2, 2, P], F32, tag="z0T")
-                for s in range(2):
-                    z0_words = z0_sb[j][:, 2 * h + s, :].bitcast(F32)
-                    for u in range(2):
-                        nc.tensor.transpose(
-                            z0T_ps[:, s, u, :], z0_words[:, u : D // 2 : 2], ident_f32[:]
-                        )
-                nc.scalar.copy(
-                    out=words[:, h], in_=z0T_ps[:].rearrange("p s u b -> p s b u")
-                )
-            z0_grouped[j] = grouped
+        def transpose_z0(pair):
+            j, h = divmod(pair, 2)
+            bank = psum_t.tile([P, 2, 2, P], F32, tag="t")
+            for s in range(2):
+                transpose_words(bank, s, z0_sb[j][:, 2 * h + s, :])
+            z0T[pair] = bank
 
-        def quantise_z0(j):
-            codes = z0q_pool.tile([P, BLOCK], U32, name="z0_codes", align_bytes=64)
-            scales = z0q_pool.tile([P, BLOCK], U8, name="z0_scales", align_bytes=64)
+        def interleave_z0(pair, engine):
+            grouped = stage.tile([P, 2 * P * PACK], BF16, name="z0_grouped", align_bytes=64)
+            interleave(engine, grouped[:], z0T[pair])
+            z0_grouped[pair] = grouped
+
+        def quantise_z0(pair):
+            codes = stage.tile([P, 2 * P], U32, name="z0_codes", align_bytes=64)
+            scales = stage.tile([P, 2 * P], U8, name="z0_scales", align_bytes=64)
             nc.vector.quantize_mx(
-                out=codes[:].bitcast(FP8X4), scales=scales[:], in_=z0_grouped[j][:]
+                out=codes[:].bitcast(FP8X4), scales=scales[:], in_=z0_grouped[pair][:]
             )
-            z0_codes[j] = codes
-            z0_scales[j] = scales
+            z0_codes[pair] = codes
+            z0_scales[pair] = scales
 
+        cb_grouped = const.tile([P, K * PACK], BF16, align_bytes=64)
         cb_codes = const.tile([P, K], U32, align_bytes=64)
         cb_scales = const.tile([P, K], U8, align_bytes=64)
         c_sq = const.tile([P, K], F32)
+        c_sq_by_partition = const.tile([P, CB_TILES], F32)
 
         def prepare_codebook():
-            grouped = const.tile([P, K, PACK], BF16, name="cb_grouped", align_bytes=64)
             for pair in range(CB_TILES // 2):
-                cbT_ps = psum.tile([P, 2, PACK, P], BF16, tag="dist")
+                bank = psum_d.tile([P, 2, 2, P], F32, tag="d")
                 for r in range(2):
-                    for t in range(PACK):
-                        nc.tensor.transpose(
-                            cbT_ps[:, r, t, :],
-                            cb_sb[:, 2 * pair + r, t * P : (t + 1) * P],
-                            ident_bf16[:],
-                        )
-                nc.vector.tensor_scalar_mul(
-                    out=grouped[:, 2 * pair * P : (2 * pair + 2) * P, :].rearrange(
-                        "p (r k) t -> p r k t", r=2
-                    ),
-                    in0=cbT_ps[:].rearrange("p r t k -> p r k t"),
-                    scalar1=-2.0,
-                )
+                    transpose_words(bank, r, cb_sb[:, 2 * pair + r, :])
+                columns = slice(2 * pair * P * PACK, (2 * pair + 2) * P * PACK)
+                interleave("vector", cb_grouped[:, columns], bank)
             for h in range(CODE_HALVES):
                 half = slice(h * BANK, (h + 1) * BANK)
                 nc.vector.quantize_mx(
                     out=cb_codes[:, half].bitcast(FP8X4),
                     scales=cb_scales[:, half],
-                    in_=grouped[:, half, :].rearrange("p k t -> p (k t)"),
+                    in_=cb_grouped[:, h * BANK * PACK : (h + 1) * BANK * PACK],
                 )
-
-        c_sq_by_partition = const.tile([P, CB_TILES], F32)
 
         def square_codebook():
             for r in range(CB_TILES):
@@ -158,7 +163,7 @@ def tile_softresidualvq_pa_t_kernel(tc, z0, W_words, W_scales, cb, out_0, out_1)
                 in_=c_sq_by_partition[:].unsqueeze(2).to_broadcast([P, CB_TILES, P]),
             )
             for h in range(CODE_HALVES):
-                c_sq_ps = psum.tile([P, BANK // P, P], F32, tag="z")
+                c_sq_ps = psum_d.tile([P, BANK // P, P], F32, tag="d")
                 for r in range(BANK // P):
                     nc.tensor.transpose(
                         c_sq_ps[:, r, :], repeated[:, h * (BANK // P) + r, :], ident_f32[:]
@@ -168,109 +173,147 @@ def tile_softresidualvq_pa_t_kernel(tc, z0, W_words, W_scales, cb, out_0, out_1)
                     in_=c_sq_ps[:].rearrange("p r k -> p (r k)"),
                 )
 
+        z_ps = {}
         z_out = {}
         z_sq = {}
-        z_grouped = {}
-        z_codes = {}
-        z_scales = {}
+        z_bf16 = {}
 
-        def whiten_tile(tau):
-            j, s = divmod(tau, TILES_PER_BLOCK)
+        def whiten(tau):
+            pair, s = divmod(tau, 2)
             rows = slice(s * P, (s + 1) * P)
-            if s == 0:
-                z_out[j] = out_pool.tile([P, TILES_PER_BLOCK, D], F32, name="z_out")
-                z_sq[j] = out_pool.tile([P, TILES_PER_BLOCK], F32, name="z_sq")
-
-            zT_ps = psum.tile([P, PACK, P], F32, tag="zT")
-            for t in range(PACK):
-                nc.tensor.matmul_mx(
-                    out=zT_ps[:, t, :],
-                    lhsT=w_words[:, 2 * t * P : 2 * (t + 1) * P].bitcast(FP4X4),
-                    lhsT_scale=w_scales[:, t * P : (t + 1) * P],
-                    rhs=z0_codes[j][:, rows].bitcast(FP8X4),
-                    rhs_scale=z0_scales[j][:, rows],
-                    start=True,
-                    stop=True,
-                )
-            grouped = zq_pool.tile([P, P, PACK], BF16, name="z_grouped", align_bytes=64)
-            if tau % 2 == 0:
-                nc.scalar.copy(out=grouped[:], in_=zT_ps[:].rearrange("p t b -> p b t"))
-            else:
-                nc.vector.tensor_copy(out=grouped[:], in_=zT_ps[:].rearrange("p t b -> p b t"))
-            z_grouped[tau] = grouped
-
-            z_ps = psum.tile([P, D], F32, tag="z")
+            bank = psum_z.tile([P, D], F32, tag="z")
             nc.tensor.matmul_mx(
-                out=z_ps[:],
-                lhsT=z0_codes[j][:, rows].bitcast(FP8X4),
-                lhsT_scale=z0_scales[j][:, rows],
+                out=bank[:],
+                lhsT=z0_codes[pair][:, rows].bitcast(FP8X4),
+                lhsT_scale=z0_scales[pair][:, rows],
                 rhs=w_words[:].bitcast(FP4X4),
                 rhs_scale=w_scales[:],
                 start=True,
                 stop=True,
             )
-            nc.scalar.copy(out=z_out[j][:, s, :], in_=z_ps[:])
+            z_ps[tau] = bank
+
+        def copy_z(tau, engine):
+            j, s = divmod(tau, TILES_PER_BLOCK)
+            if s == 0:
+                z_out[j] = out_pool.tile([P, TILES_PER_BLOCK, D], F32, name="z_out")
+                z_sq[j] = out_pool.tile([P, TILES_PER_BLOCK], F32, name="z_sq")
+            copy_on(engine, z_out[j][:, s, :], z_ps[tau][:])
+            rounded = zb_pool.tile([P, D], BF16, name="z_bf16")
+            nc.gpsimd.tensor_scalar(
+                out=rounded[:].rearrange("p (u q e) -> p u q e", u=2, e=2),
+                in0=z_out[j][:, s, :].rearrange("p (q u e) -> p u q e", u=2, e=2),
+                scalar1=-2.0,
+                scalar2=0.0,
+                op0=MULT,
+                op1=ADD,
+            )
+            z_bf16[tau] = rounded
+
+        def square_z(tau):
+            j, s = divmod(tau, TILES_PER_BLOCK)
             squares = scratch.tile([P, D], F32, name="squares")
             nc.scalar.activation(
-                out=squares[:], in_=z_ps[:], func=SQUARE, accum_out=z_sq[j][:, s : s + 1]
+                out=squares[:], in_=z_ps[tau][:], func=SQUARE, accum_out=z_sq[j][:, s : s + 1]
             )
-            store_finished_tiles(out_0, z_out[j], j, s)
 
-        def quantise_z(tau):
-            codes = zq_pool.tile([P, P], U32, name="z_codes", align_bytes=64)
-            scales = zq_pool.tile([P, P], U8, name="z_scales", align_bytes=64)
+        zT = {}
+        z_grouped = {}
+        z_codes = {}
+        z_scales = {}
+
+        def transpose_z(pair):
+            bank = psum_t.tile([P, 2, 2, P], F32, tag="t")
+            for s in range(2):
+                words = z_bf16[2 * pair + s][:].bitcast(F32)
+                for u in range(2):
+                    nc.tensor.transpose(bank[:, s, u, :], words[:, u * P : (u + 1) * P], ident_f32[:])
+            zT[pair] = bank
+
+        def interleave_z(pair, engine):
+            grouped = stage.tile([P, 2 * P * PACK], BF16, name="z_grouped", align_bytes=64)
+            interleave(engine, grouped[:], zT[pair])
+            z_grouped[pair] = grouped
+
+        def quantise_z(pair):
+            codes = stage.tile([P, 2 * P], U32, name="z_codes", align_bytes=64)
+            scales = stage.tile([P, 2 * P], U8, name="z_scales", align_bytes=64)
             nc.vector.quantize_mx(
-                out=codes[:].bitcast(FP8X4),
-                scales=scales[:],
-                in_=z_grouped[tau][:].rearrange("p b t -> p (b t)"),
+                out=codes[:].bitcast(FP8X4), scales=scales[:], in_=z_grouped[pair][:]
             )
-            z_codes[tau] = codes
-            z_scales[tau] = scales
+            z_codes[pair] = codes
+            z_scales[pair] = scales
 
         d_out = {}
 
         def distance_tile(tau):
             j, s = divmod(tau, TILES_PER_BLOCK)
+            pair, t = divmod(tau, 2)
+            rows = slice(t * P, (t + 1) * P)
             if s == 0:
                 d_out[j] = out_pool.tile([P, TILES_PER_BLOCK, K], F32, name="d_out")
+            banks = []
             for h in range(CODE_HALVES):
                 half = slice(h * BANK, (h + 1) * BANK)
-                dist_ps = psum.tile([P, BANK], F32, tag="dist")
+                dist_ps = psum_d.tile([P, BANK], F32, tag="d")
                 nc.tensor.matmul_mx(
                     out=dist_ps[:],
-                    lhsT=z_codes[tau][:].bitcast(FP8X4),
-                    lhsT_scale=z_scales[tau][:],
+                    lhsT=z_codes[pair][:, rows].bitcast(FP8X4),
+                    lhsT_scale=z_scales[pair][:, rows],
                     rhs=cb_codes[:, half].bitcast(FP8X4),
                     rhs_scale=cb_scales[:, half],
                     start=True,
                     stop=True,
                 )
+                banks.append(dist_ps)
+            for h in range(CODE_HALVES):
+                half = slice(h * BANK, (h + 1) * BANK)
                 nc.vector.scalar_tensor_tensor(
                     out=d_out[j][:, s, half],
-                    in0=dist_ps[:],
+                    in0=banks[h][:],
                     scalar=z_sq[j][:, s : s + 1],
                     in1=c_sq[:, half],
                     op0=ADD,
                     op1=ADD,
                 )
-            store_finished_tiles(out_1, d_out[j], j, s)
+            if tau >= N_TILES - 2:
+                store_tiles(out_1, d_out[j], j, s, s)
+            elif s % 2 == 1:
+                store_tiles(out_1, d_out[j], j, s - 1, s)
 
         with tc.manual_schedule():
-            transpose_block(0)
+            transpose_z0(0)
+            interleave_z0(0, "scalar")
             quantise_z0(0)
-            prepare_codebook()
-            square_codebook()
-            for tau in range(N_TILES + LAG):
-                j, s = divmod(tau, TILES_PER_BLOCK)
-                if s == 0 and j + 1 < N_BLOCKS:
-                    transpose_block(j + 1)
-                if tau < N_TILES:
-                    whiten_tile(tau)
-                if s == TILES_PER_BLOCK - 1 and j + 1 < N_BLOCKS:
-                    quantise_z0(j + 1)
-                if 1 <= tau <= N_TILES:
-                    quantise_z(tau - 1)
-                if tau == LAG:
+            for k in range(N_PAIRS + 2):
+                ahead, here, back, far = k + 1, k, k - 1, k - 2
+                if ahead < N_PAIRS:
+                    transpose_z0(ahead)
+                if 0 <= back < N_PAIRS:
+                    transpose_z(back)
+                if ahead < N_PAIRS:
+                    interleave_z0(ahead, "vector" if ahead < 4 else "scalar")
+                if 0 <= back < N_PAIRS:
+                    on_vector = back < 2 or (back % 3 == 0 and back < 13)
+                    interleave_z(back, "vector" if on_vector else "scalar")
+                if here < N_PAIRS:
+                    whiten(2 * here)
+                    whiten(2 * here + 1)
+                    copy_z(2 * here, "scalar")
+                    copy_z(2 * here + 1, "vector" if here < 2 else "scalar")
+                    square_z(2 * here)
+                    square_z(2 * here + 1)
+                    j, h = divmod(here, 2)
+                    store_tiles(out_0, z_out[j], j, 2 * h, 2 * h + 1)
+                if k == 0:
+                    prepare_codebook()
+                    square_codebook()
+                if ahead < N_PAIRS:
+                    quantise_z0(ahead)
+                if 0 <= back < N_PAIRS:
+                    quantise_z(back)
+                if k == 2:
                     spread_code_norms()
-                if tau >= LAG:
-                    distance_tile(tau - LAG)
+                if 0 <= far < N_PAIRS:
+                    distance_tile(2 * far)
+                    distance_tile(2 * far + 1)

@@ -35,8 +35,8 @@ def tile_softresidualvq_pa_t_kernel(tc, z0, W_words, W_scales, cb, out_0, out_1)
     with ExitStack() as ctx:
         const = ctx.enter_context(tc.tile_pool(name="const", bufs=1))
         z0_pool = ctx.enter_context(tc.tile_pool(name="z0", bufs=N_BLOCKS))
-        stage = ctx.enter_context(tc.tile_pool(name="stage", bufs=3))
-        zb_pool = ctx.enter_context(tc.tile_pool(name="zb", bufs=6))
+        stage = ctx.enter_context(tc.tile_pool(name="stage", bufs=4))
+        zb_pool = ctx.enter_context(tc.tile_pool(name="zb", bufs=8))
         out_pool = ctx.enter_context(tc.tile_pool(name="out", bufs=3))
         scratch = ctx.enter_context(tc.tile_pool(name="scratch", bufs=4))
         psum_t = ctx.enter_context(tc.psum_pool(name="psum_t", bufs=2))
@@ -285,8 +285,8 @@ def tile_softresidualvq_pa_t_kernel(tc, z0, W_words, W_scales, cb, out_0, out_1)
             transpose_z0(0)
             interleave_z0(0, "scalar")
             quantise_z0(0)
-            for k in range(N_PAIRS + 2):
-                ahead, here, back, far = k + 1, k, k - 1, k - 2
+            for k in range(N_PAIRS + 3):
+                ahead, here, back, far = k + 1, k, k - 2, k - 3
                 if ahead < N_PAIRS:
                     transpose_z0(ahead)
                 if 0 <= back < N_PAIRS:
@@ -312,7 +312,7 @@ def tile_softresidualvq_pa_t_kernel(tc, z0, W_words, W_scales, cb, out_0, out_1)
                     quantise_z0(ahead)
                 if 0 <= back < N_PAIRS:
                     quantise_z(back)
-                if k == 2:
+                if k == 3:
                     spread_code_norms()
                 if 0 <= far < N_PAIRS:
                     distance_tile(2 * far)

@@ -276,10 +276,12 @@ def tile_softresidualvq_pa_t_kernel(tc, z0, W_words, W_scales, cb, out_0, out_1)
                     op0=ADD,
                     op1=ADD,
                 )
-            if tau >= N_TILES - 2:
+                if tau == N_TILES - 1:
+                    nc.sync.dma_start(
+                        out=block_rows(out_1, j)[:, s, half], in_=d_out[j][:, s, half]
+                    )
+            if tau < N_TILES - 1:
                 store_tiles(out_1, d_out[j], j, s, s)
-            elif s % 2 == 1:
-                store_tiles(out_1, d_out[j], j, s - 1, s)
 
         with tc.manual_schedule():
             transpose_z0(0)

@@ -157,16 +157,16 @@ def tile_softresidualvq_pa_t_kernel(tc, z0, W_words, W_scales, cb, out_0, out_1)
                 )
 
         def spread_code_norms():
-            repeated = const.tile([P, CB_TILES, P], F32, name="c_sq_repeated")
-            nc.vector.tensor_copy(
-                out=repeated[:],
-                in_=c_sq_by_partition[:].unsqueeze(2).to_broadcast([P, CB_TILES, P]),
-            )
             for h in range(CODE_HALVES):
                 c_sq_ps = psum_d.tile([P, BANK // P, P], F32, tag="d")
                 for r in range(BANK // P):
-                    nc.tensor.transpose(
-                        c_sq_ps[:, r, :], repeated[:, h * (BANK // P) + r, :], ident_f32[:]
+                    column = h * (BANK // P) + r
+                    nc.tensor.matmul(
+                        out=c_sq_ps[:, r, :],
+                        lhsT=c_sq_by_partition[:, column : column + 1].to_broadcast([P, P]),
+                        rhs=ident_f32[:],
+                        start=True,
+                        stop=True,
                     )
                 nc.vector.tensor_copy(
                     out=c_sq[:, h * BANK : (h + 1) * BANK],
@@ -296,13 +296,13 @@ def tile_softresidualvq_pa_t_kernel(tc, z0, W_words, W_scales, cb, out_0, out_1)
                 if ahead < N_PAIRS:
                     interleave_z0(ahead, "vector" if ahead < 4 else "scalar")
                 if 0 <= back < N_PAIRS:
-                    on_vector = back < 2 or (back % 3 == 0 and back < 13)
+                    on_vector = back < 2 or (back % 2 == 1 and back < 13)
                     interleave_z(back, "vector" if on_vector else "scalar")
                 if here < N_PAIRS:
                     whiten(2 * here)
                     whiten(2 * here + 1)
                     copy_z(2 * here, "scalar")
-                    copy_z(2 * here + 1, "vector" if here < 2 else "scalar")
+                    copy_z(2 * here + 1, "vector" if here < 3 else "scalar")
                     square_z(2 * here)
                     square_z(2 * here + 1)
                     j, h = divmod(here, 2)

@@ -131,47 +131,45 @@ def tile_softresidualvq_pa_t_kernel(tc, z0, W_words, W_scales, cb, out_0, out_1)
         c_sq = const.tile([P, K], F32)
         c_sq_by_partition = const.tile([P, CB_TILES], F32)
 
-        def prepare_codebook():
-            for pair in range(CB_TILES // 2):
-                bank = psum_d.tile([P, 2, 2, P], F32, tag="d")
-                for r in range(2):
-                    transpose_words(bank, r, cb_sb[:, 2 * pair + r, :])
-                columns = slice(2 * pair * P * PACK, (2 * pair + 2) * P * PACK)
-                interleave("vector", cb_grouped[:, columns], bank)
-            for h in range(CODE_HALVES):
-                half = slice(h * BANK, (h + 1) * BANK)
-                nc.vector.quantize_mx(
-                    out=cb_codes[:, half].bitcast(FP8X4),
-                    scales=cb_scales[:, half],
-                    in_=cb_grouped[:, h * BANK * PACK : (h + 1) * BANK * PACK],
-                )
+        def transpose_codebook(pair):
+            bank = psum_d.tile([P, 2, 2, P], F32, tag="d")
+            for r in range(2):
+                transpose_words(bank, r, cb_sb[:, 2 * pair + r, :])
+            columns = slice(2 * pair * P * PACK, (2 * pair + 2) * P * PACK)
+            interleave("vector", cb_grouped[:, columns], bank)
 
-        def square_codebook():
-            for r in range(CB_TILES):
-                squares = scratch.tile([P, D], F32, name="squares")
-                nc.scalar.activation(
-                    out=squares[:],
-                    in_=cb_sb[:, r, :],
-                    func=SQUARE,
-                    accum_out=c_sq_by_partition[:, r : r + 1],
-                )
+        def quantise_codebook(h):
+            half = slice(h * BANK, (h + 1) * BANK)
+            nc.vector.quantize_mx(
+                out=cb_codes[:, half].bitcast(FP8X4),
+                scales=cb_scales[:, half],
+                in_=cb_grouped[:, h * BANK * PACK : (h + 1) * BANK * PACK],
+            )
 
-        def spread_code_norms():
-            for h in range(CODE_HALVES):
-                c_sq_ps = psum_d.tile([P, BANK // P, P], F32, tag="d")
-                for r in range(BANK // P):
-                    column = h * (BANK // P) + r
-                    nc.tensor.matmul(
-                        out=c_sq_ps[:, r, :],
-                        lhsT=c_sq_by_partition[:, column : column + 1].to_broadcast([P, P]),
-                        rhs=ident_f32[:],
-                        start=True,
-                        stop=True,
-                    )
-                nc.vector.tensor_copy(
-                    out=c_sq[:, h * BANK : (h + 1) * BANK],
-                    in_=c_sq_ps[:].rearrange("p r k -> p (r k)"),
+        def square_codebook(r):
+            squares = scratch.tile([P, D], F32, name="squares")
+            nc.scalar.activation(
+                out=squares[:],
+                in_=cb_sb[:, r, :],
+                func=SQUARE,
+                accum_out=c_sq_by_partition[:, r : r + 1],
+            )
+
+        def spread_code_norms(h):
+            c_sq_ps = psum_d.tile([P, BANK // P, P], F32, tag="d")
+            for r in range(BANK // P):
+                column = h * (BANK // P) + r
+                nc.tensor.matmul(
+                    out=c_sq_ps[:, r, :],
+                    lhsT=c_sq_by_partition[:, column : column + 1].to_broadcast([P, P]),
+                    rhs=ident_f32[:],
+                    start=True,
+                    stop=True,
                 )
+            nc.vector.tensor_copy(
+                out=c_sq[:, h * BANK : (h + 1) * BANK],
+                in_=c_sq_ps[:].rearrange("p r k -> p (r k)"),
+            )
 
         z_ps = {}
         z_out = {}
@@ -307,15 +305,28 @@ def tile_softresidualvq_pa_t_kernel(tc, z0, W_words, W_scales, cb, out_0, out_1)
                     square_z(2 * here + 1)
                     j, h = divmod(here, 2)
                     store_tiles(out_0, z_out[j], j, 2 * h, 2 * h + 1)
-                if k == 0:
-                    prepare_codebook()
-                    square_codebook()
                 if ahead < N_PAIRS:
                     quantise_z0(ahead)
                 if 0 <= back < N_PAIRS:
                     quantise_z(back)
+                if k == 0:
+                    transpose_codebook(0)
+                    transpose_codebook(1)
+                    for r in (0, 1, 2):
+                        square_codebook(r)
+                if k == 1:
+                    transpose_codebook(2)
+                    transpose_codebook(3)
+                    quantise_codebook(0)
+                    for r in (3, 4, 5):
+                        square_codebook(r)
+                if k == 2:
+                    quantise_codebook(1)
+                    spread_code_norms(0)
+                    for r in (6, 7):
+                        square_codebook(r)
                 if k == 3:
-                    spread_code_norms()
+                    spread_code_norms(1)
                 if 0 <= far < N_PAIRS:
                     distance_tile(2 * far)
                     distance_tile(2 * far + 1)

@@ -212,7 +212,10 @@ def tile_softresidualvq_pa_t_kernel(tc, z0, W_words, W_scales, cb, out_0, out_1)
             j, s = divmod(tau, TILES_PER_BLOCK)
             squares = scratch.tile([P, D], F32, name="squares")
             nc.scalar.activation(
-                out=squares[:], in_=z_ps[tau][:], func=SQUARE, accum_out=z_sq[j][:, s : s + 1]
+                out=squares[:],
+                in_=z_out[j][:, s, :],
+                func=SQUARE,
+                accum_out=z_sq[j][:, s : s + 1],
             )
 
         zT = {}
@@ -292,7 +295,7 @@ def tile_softresidualvq_pa_t_kernel(tc, z0, W_words, W_scales, cb, out_0, out_1)
                 if 0 <= back < N_PAIRS:
                     transpose_z(back)
                 if ahead < N_PAIRS:
-                    interleave_z0(ahead, "vector" if ahead < 4 else "scalar")
+                    interleave_z0(ahead, "vector" if ahead < 3 else "scalar")
                 if 0 <= back < N_PAIRS:
                     on_vector = back < 2 or (back % 2 == 1 and back < 13)
                     interleave_z(back, "vector" if on_vector else "scalar")
@@ -301,10 +304,11 @@ def tile_softresidualvq_pa_t_kernel(tc, z0, W_words, W_scales, cb, out_0, out_1)
                     whiten(2 * here + 1)
                     copy_z(2 * here, "scalar")
                     copy_z(2 * here + 1, "vector" if here < 3 else "scalar")
-                    square_z(2 * here)
-                    square_z(2 * here + 1)
                     j, h = divmod(here, 2)
                     store_tiles(out_0, z_out[j], j, 2 * h, 2 * h + 1)
+                if 0 <= back < N_PAIRS:
+                    square_z(2 * back)
+                    square_z(2 * back + 1)
                 if ahead < N_PAIRS:
                     quantise_z0(ahead)
                 if 0 <= back < N_PAIRS:

from contextlib import ExitStack

import concourse.mybir as mybir
from concourse.masks import make_identity

F32 = mybir.dt.float32
BF16 = mybir.dt.bfloat16
I32 = mybir.dt.int32
U32 = mybir.dt.uint32
U8 = mybir.dt.uint8
FP8X4 = mybir.dt.float8_e4m3fn_x4
FP4X4 = mybir.dt.float4_e2m1fn_x4
ADD = mybir.AluOpType.add
MULT = mybir.AluOpType.mult
SQUARE = mybir.ActivationFunctionType.Square

P = 128
PACK = 4
B, D, K = 4096, 512, 1024
BANK = 512
TILES_PER_BLOCK = 4
BLOCK = P * TILES_PER_BLOCK
N_BLOCKS = B // BLOCK
N_TILES = B // P
N_PAIRS = N_TILES // 2
CB_TILES = K // P
CODE_HALVES = K // BANK
WORDS = D // 2

FLOPS = 2 * B * D * D + 2 * B * D * K


def tile_softresidualvq_pa_t_kernel(tc, z0, W_words, W_scales, cb, out_0, out_1):
    nc = tc.nc
    with ExitStack() as ctx:
        const = ctx.enter_context(tc.tile_pool(name="const", bufs=1))
        z0_pool = ctx.enter_context(tc.tile_pool(name="z0", bufs=N_BLOCKS))
        stage = ctx.enter_context(tc.tile_pool(name="stage", bufs=4))
        zb_pool = ctx.enter_context(tc.tile_pool(name="zb", bufs=8))
        out_pool = ctx.enter_context(tc.tile_pool(name="out", bufs=3))
        scratch = ctx.enter_context(tc.tile_pool(name="scratch", bufs=4))
        psum_t = ctx.enter_context(tc.psum_pool(name="psum_t", bufs=2))
        psum_z = ctx.enter_context(tc.psum_pool(name="psum_z", bufs=2))
        psum_d = ctx.enter_context(tc.psum_pool(name="psum_d", bufs=4))

        def block_rows(dram, j):
            return dram[j * BLOCK : (j + 1) * BLOCK, :].rearrange(
                "(p s) d -> p s d", s=TILES_PER_BLOCK
            )

        def store_tiles(dram, block_sb, j, first, last):
            tiles = slice(first, last + 1)
            nc.sync.dma_start(out=block_rows(dram, j)[:, tiles, :], in_=block_sb[:, tiles, :])

        z0_sb = {}

        def load_z0(j, pieces):
            rows = z0_pool.tile([P, TILES_PER_BLOCK, D], BF16, name="z0_rows")
            step = TILES_PER_BLOCK // pieces
            for c in range(pieces):
                tiles = slice(c * step, (c + 1) * step)
                nc.sync.dma_start(out=rows[:, tiles, :], in_=block_rows(z0, j)[:, tiles, :])
            z0_sb[j] = rows

        w_words = const.tile([P, 2 * D], U8, align_bytes=64)
        w_scales = const.tile([P, D], U8, align_bytes=64)
        nc.vector.memset(w_scales[:].bitcast(I32), 0)

        load_z0(0, 2)
        nc.sync.dma_start(out=w_words[:].bitcast(I32), in_=W_words[0].bitcast(I32))
        for q in range(4):
            nc.sync.dma_start(
                out=w_scales[32 * q : 32 * q + 4, :].bitcast(I32),
                in_=W_scales[0, 4 * q : 4 * q + 4, :].bitcast(I32),
            )
        cb_sb = const.tile([P, CB_TILES, D], BF16)
        nc.sync.dma_start(out=cb_sb[:], in_=cb.rearrange("(r p) d -> p r d", p=P))
        for j in range(1, N_BLOCKS):
            load_z0(j, 1)

        ident_f32 = const.tile([P, P], F32)
        make_identity(nc, ident_f32[:])

        def copy_on(engine, out, in_):
            if engine == "scalar":
                nc.scalar.copy(out=out, in_=in_)
            else:
                nc.vector.tensor_copy(out=out, in_=in_)

        def transpose_words(bank, slot, rows_bf16):
            words = rows_bf16.bitcast(F32)
            for u in range(2):
                nc.tensor.transpose(bank[:, slot, u, :], words[:, u:WORDS:2], ident_f32[:])

        def interleave(engine, grouped_bf16, bank):
            copy_on(
                engine,
                grouped_bf16.bitcast(F32).rearrange("p (s b u) -> p s b u", s=2, u=2),
                bank[:].rearrange("p s u b -> p s b u"),
            )

        z0T = {}
        z0_grouped = {}
        z0_codes = {}
        z0_scales = {}

        def transpose_z0(pair):
            j, h = divmod(pair, 2)
            bank = psum_t.tile([P, 2, 2, P], F32, tag="t")
            for s in range(2):
                transpose_words(bank, s, z0_sb[j][:, 2 * h + s, :])
            z0T[pair] = bank

        def interleave_z0(pair, engine):
            grouped = stage.tile([P, 2 * P * PACK], BF16, name="z0_grouped", align_bytes=64)
            interleave(engine, grouped[:], z0T[pair])
            z0_grouped[pair] = grouped

        def quantise_z0(pair):
            codes = stage.tile([P, 2 * P], U32, name="z0_codes", align_bytes=64)
            scales = stage.tile([P, 2 * P], U8, name="z0_scales", align_bytes=64)
            nc.vector.quantize_mx(
                out=codes[:].bitcast(FP8X4), scales=scales[:], in_=z0_grouped[pair][:]
            )
            z0_codes[pair] = codes
            z0_scales[pair] = scales

        cb_grouped = const.tile([P, K * PACK], BF16, align_bytes=64)
        cb_codes = const.tile([P, K], U32, align_bytes=64)
        cb_scales = const.tile([P, K], U8, align_bytes=64)
        c_sq = const.tile([P, K], F32)
        c_sq_by_partition = const.tile([P, CB_TILES], F32)

        def transpose_codebook(pair):
            bank = psum_d.tile([P, 2, 2, P], F32, tag="d")
            for r in range(2):
                transpose_words(bank, r, cb_sb[:, 2 * pair + r, :])
            columns = slice(2 * pair * P * PACK, (2 * pair + 2) * P * PACK)
            interleave("vector", cb_grouped[:, columns], bank)

        def quantise_codebook(h):
            half = slice(h * BANK, (h + 1) * BANK)
            nc.vector.quantize_mx(
                out=cb_codes[:, half].bitcast(FP8X4),
                scales=cb_scales[:, half],
                in_=cb_grouped[:, h * BANK * PACK : (h + 1) * BANK * PACK],
            )

        def square_codebook(r):
            squares = scratch.tile([P, D], F32, name="squares")
            nc.scalar.activation(
                out=squares[:],
                in_=cb_sb[:, r, :],
                func=SQUARE,
                accum_out=c_sq_by_partition[:, r : r + 1],
            )

        def spread_code_norms(h):
            c_sq_ps = psum_d.tile([P, BANK // P, P], F32, tag="d")
            for r in range(BANK // P):
                column = h * (BANK // P) + r
                nc.tensor.matmul(
                    out=c_sq_ps[:, r, :],
                    lhsT=c_sq_by_partition[:, column : column + 1].to_broadcast([P, P]),
                    rhs=ident_f32[:],
                    start=True,
                    stop=True,
                )
            nc.vector.tensor_copy(
                out=c_sq[:, h * BANK : (h + 1) * BANK],
                in_=c_sq_ps[:].rearrange("p r k -> p (r k)"),
            )

        z_ps = {}
        z_out = {}
        z_sq = {}
        z_bf16 = {}

        def whiten(tau):
            pair, s = divmod(tau, 2)
            rows = slice(s * P, (s + 1) * P)
            bank = psum_z.tile([P, D], F32, tag="z")
            nc.tensor.matmul_mx(
                out=bank[:],
                lhsT=z0_codes[pair][:, rows].bitcast(FP8X4),
                lhsT_scale=z0_scales[pair][:, rows],
                rhs=w_words[:].bitcast(FP4X4),
                rhs_scale=w_scales[:],
                start=True,
                stop=True,
            )
            z_ps[tau] = bank

        def copy_z(tau, engine):
            j, s = divmod(tau, TILES_PER_BLOCK)
            if s == 0:
                z_out[j] = out_pool.tile([P, TILES_PER_BLOCK, D], F32, name="z_out")
                z_sq[j] = out_pool.tile([P, TILES_PER_BLOCK], F32, name="z_sq")
            copy_on(engine, z_out[j][:, s, :], z_ps[tau][:])
            rounded = zb_pool.tile([P, D], BF16, name="z_bf16")
            nc.gpsimd.tensor_scalar(
                out=rounded[:].rearrange("p (u q e) -> p u q e", u=2, e=2),
                in0=z_out[j][:, s, :].rearrange("p (q u e) -> p u q e", u=2, e=2),
                scalar1=-2.0,
                scalar2=0.0,
                op0=MULT,
                op1=ADD,
            )
            z_bf16[tau] = rounded

        def square_z(tau):
            j, s = divmod(tau, TILES_PER_BLOCK)
            squares = scratch.tile([P, D], F32, name="squares")
            nc.scalar.activation(
                out=squares[:],
                in_=z_out[j][:, s, :],
                func=SQUARE,
                accum_out=z_sq[j][:, s : s + 1],
            )

        zT = {}
        z_grouped = {}
        z_codes = {}
        z_scales = {}

        def transpose_z(pair):
            bank = psum_t.tile([P, 2, 2, P], F32, tag="t")
            for s in range(2):
                words = z_bf16[2 * pair + s][:].bitcast(F32)
                for u in range(2):
                    nc.tensor.transpose(bank[:, s, u, :], words[:, u * P : (u + 1) * P], ident_f32[:])
            zT[pair] = bank

        def interleave_z(pair, engine):
            grouped = stage.tile([P, 2 * P * PACK], BF16, name="z_grouped", align_bytes=64)
            interleave(engine, grouped[:], zT[pair])
            z_grouped[pair] = grouped

        def quantise_z(pair):
            codes = stage.tile([P, 2 * P], U32, name="z_codes", align_bytes=64)
            scales = stage.tile([P, 2 * P], U8, name="z_scales", align_bytes=64)
            nc.vector.quantize_mx(
                out=codes[:].bitcast(FP8X4), scales=scales[:], in_=z_grouped[pair][:]
            )
            z_codes[pair] = codes
            z_scales[pair] = scales

        d_out = {}

        def distance_tile(tau):
            j, s = divmod(tau, TILES_PER_BLOCK)
            pair, t = divmod(tau, 2)
            rows = slice(t * P, (t + 1) * P)
            if s == 0:
                d_out[j] = out_pool.tile([P, TILES_PER_BLOCK, K], F32, name="d_out")
            banks = []
            for h in range(CODE_HALVES):
                half = slice(h * BANK, (h + 1) * BANK)
                dist_ps = psum_d.tile([P, BANK], F32, tag="d")
                nc.tensor.matmul_mx(
                    out=dist_ps[:],
                    lhsT=z_codes[pair][:, rows].bitcast(FP8X4),
                    lhsT_scale=z_scales[pair][:, rows],
                    rhs=cb_codes[:, half].bitcast(FP8X4),
                    rhs_scale=cb_scales[:, half],
                    start=True,
                    stop=True,
                )
                banks.append(dist_ps)
            for h in range(CODE_HALVES):
                half = slice(h * BANK, (h + 1) * BANK)
                nc.vector.scalar_tensor_tensor(
                    out=d_out[j][:, s, half],
                    in0=banks[h][:],
                    scalar=z_sq[j][:, s : s + 1],
                    in1=c_sq[:, half],
                    op0=ADD,
                    op1=ADD,
                )
                if tau == N_TILES - 1:
                    nc.sync.dma_start(
                        out=block_rows(out_1, j)[:, s, half], in_=d_out[j][:, s, half]
                    )
            if tau < N_TILES - 1:
                store_tiles(out_1, d_out[j], j, s, s)

        with tc.manual_schedule():
            transpose_z0(0)
            interleave_z0(0, "scalar")
            quantise_z0(0)
            for k in range(N_PAIRS + 3):
                ahead, here, back, far = k + 1, k, k - 2, k - 3
                if ahead < N_PAIRS:
                    transpose_z0(ahead)
                if 0 <= back < N_PAIRS:
                    transpose_z(back)
                if ahead < N_PAIRS:
                    interleave_z0(ahead, "vector" if ahead < 3 else "scalar")
                if 0 <= back < N_PAIRS:
                    on_vector = back < 2 or (back % 2 == 1 and back < 13)
                    interleave_z(back, "vector" if on_vector else "scalar")
                if here < N_PAIRS:
                    whiten(2 * here)
                    whiten(2 * here + 1)
                    copy_z(2 * here, "scalar")
                    copy_z(2 * here + 1, "vector" if here < 3 else "scalar")
                    j, h = divmod(here, 2)
                    store_tiles(out_0, z_out[j], j, 2 * h, 2 * h + 1)
                if 0 <= back < N_PAIRS:
                    square_z(2 * back)
                    square_z(2 * back + 1)
                if ahead < N_PAIRS:
                    quantise_z0(ahead)
                if 0 <= back < N_PAIRS:
                    quantise_z(back)
                if k == 0:
                    transpose_codebook(0)
                    transpose_codebook(1)
                    for r in (0, 1, 2):
                        square_codebook(r)
                if k == 1:
                    transpose_codebook(2)
                    transpose_codebook(3)
                    quantise_codebook(0)
                    for r in (3, 4, 5):
                        square_codebook(r)
                if k == 2:
                    quantise_codebook(1)
                    spread_code_norms(0)
                    for r in (6, 7):
                        square_codebook(r)
                if k == 3:
                    spread_code_norms(1)
                if 0 <= far < N_PAIRS:
                    distance_tile(2 * far)
                    distance_tile(2 * far + 1)
